import numpy as np
import ml_dtypes


def mxq(x, axis, fmt="e4m3"):
    dtype, down = {"e4m3": (ml_dtypes.float8_e4m3fn, 7), "e5m2": (ml_dtypes.float8_e5m2, 14)}[fmt]
    v = np.moveaxis(np.asarray(x, np.float32).astype(ml_dtypes.bfloat16).astype(np.float64), axis, -1)
    blocks = v.reshape(v.shape[:-1] + (-1, 32))
    amax = np.abs(blocks).max(-1, keepdims=True)
    byte = np.maximum(np.where(amax > 0, np.frexp(amax)[1] - 1 + 127, 0) - down, 1)
    scale = np.exp2(byte - 127.0)
    codes = (blocks / scale).astype(np.float32).astype(dtype).astype(np.float64)
    return np.moveaxis((codes * scale).reshape(v.shape), -1, axis)


WIDE = False


def mx_kscale(k):
    if not WIDE:
        return np.ones(k)
    levels = np.array([10, -10, 5, -5, 0])
    if k % 512:
        return np.exp2(np.random.permutation(np.resize(levels, k // 32))).repeat(32)
    a = np.empty((k // 512, 16))
    for p in range(k // 512):
        a[p, :8] = np.random.permutation(np.resize(levels, 8))
        for g in range(8):
            far = levels[np.abs(levels - a[p, g]) >= 10]
            a[p, g + 8] = far[np.random.randint(len(far))]
    return np.exp2(a.ravel()).repeat(32)


BF16 = ml_dtypes.bfloat16


def bf(x):
    return np.asarray(x, np.float32).astype(BF16)


def f64(x):
    return np.asarray(x).astype(np.float64)


E2M1 = np.array([0.0, 0.5, 1.0, 1.5, 2.0, 3.0, 4.0, 6.0, -0.0, -0.5, -1.0, -1.5, -2.0, -3.0, -4.0, -6.0])


def pack_weight(w, fmt):
    k, n = w.shape
    w = f64(bf(w)).reshape(k // 32, 32, n)
    amax = np.abs(w).max(1)
    if fmt == "e4m3":
        byte = np.frexp(amax)[1] - 1 + 127 - 7
    else:
        mant, ex = np.frexp(amax / 6.0)
        byte = np.where(mant > 0.5, ex, ex - 1) + 127
    byte = np.clip(np.where(amax > 0, byte, 1), 1, 254)
    scaled = (w * np.exp2(127.0 - byte)[:, None, :]).reshape(k, n).astype(np.float32)
    by_word = np.ascontiguousarray(scaled.reshape(k // 512, 128, 4, n).transpose(0, 1, 3, 2))
    if fmt == "e4m3":
        words = by_word.astype(ml_dtypes.float8_e4m3fn).view(np.uint8)
    else:
        c = by_word.astype(ml_dtypes.float4_e2m1fn).view(np.uint8) & 0xF
        words = c[..., 0::2] | (c[..., 1::2] << 4)
    return np.ascontiguousarray(words), np.ascontiguousarray(byte.astype(np.uint8).reshape(k // 512, 16, n))


def unpack_weight(words, scales, fmt):
    g, p, n, _ = words.shape
    if fmt == "e4m3":
        vals = np.ascontiguousarray(words).view(ml_dtypes.float8_e4m3fn).astype(np.float64)
    else:
        nib = np.empty((g, p, n, 4), np.uint8)
        nib[..., 0::2] = words & 0xF
        nib[..., 1::2] = words >> 4
        vals = E2M1[nib]
    vals = vals * np.repeat(np.exp2(scales.astype(np.float64) - 127.0), 8, axis=1)[..., None]
    return vals.transpose(0, 1, 3, 2).reshape(g * 512, n)
def pack4(w):
    words, scales = pack_weight(w, "e2m1")
    return words.reshape(words.shape[0], 128, -1), scales


def unpack4(words, scales):
    return unpack_weight(words.reshape(words.shape[0], 128, -1, 2), scales, "e2m1")


B, T, U, D_ENC, D_PRED, D_JOINT, VOCAB = 4, 128, 32, 512, 512, 512, 128
LOGIT_CLAMP = 15.0


def draw0():
    se, sp = mx_kscale(D_ENC), mx_kscale(D_PRED)
    t = mx_kscale(D_JOINT)
    g = t / t.max()
    encoder_out = bf(np.random.standard_normal((B, T, D_ENC)) * se)
    predictor_out = bf(np.random.standard_normal((B, U, D_PRED)) * sp)
    W_enc_words, W_enc_scales = pack4(np.random.standard_normal((D_ENC, D_JOINT)) * 0.7 / np.sqrt(D_ENC) / se[:, None] * g)
    b_enc = bf(np.random.standard_normal(D_JOINT) * 0.2 * g)
    W_pred_words, W_pred_scales = pack4(np.random.standard_normal((D_PRED, D_JOINT)) * 0.7 / np.sqrt(D_PRED) / sp[:, None] * g)
    b_pred = bf(np.random.standard_normal(D_JOINT) * 0.2 * g)
    W_out_words, W_out_scales = pack4(np.random.standard_normal((D_JOINT, VOCAB)) * 8.0 / np.sqrt(D_JOINT) / g[:, None])
    b_out = bf(np.random.standard_normal(VOCAB) * 0.5)
    return {"encoder_out": encoder_out,
            "predictor_out": predictor_out,
            "W_enc_words": W_enc_words,
            "W_enc_scales": W_enc_scales,
            "b_enc": b_enc,
            "W_pred_words": W_pred_words,
            "W_pred_scales": W_pred_scales,
            "b_pred": b_pred,
            "W_out_words": W_out_words,
            "W_out_scales": W_out_scales,
            "b_out": b_out}


def core(encoder_out, predictor_out, W_enc_words, W_enc_scales, b_enc, W_pred_words, W_pred_scales, b_pred, W_out_words, W_out_scales, b_out):
    enc = (mxq(f64(encoder_out), 2, "e4m3") @ unpack4(W_enc_words, W_enc_scales)) + f64(b_enc)
    pred = (mxq(f64(predictor_out), 2, "e4m3") @ unpack4(W_pred_words, W_pred_scales)) + f64(b_pred)
    joint = np.tanh(enc[:, :, None, :] + pred[:, None, :, :])
    logits = (mxq(joint, 3, "e4m3") @ unpack4(W_out_words, W_out_scales)) + f64(b_out)
    return np.clip(logits, -LOGIT_CLAMP, LOGIT_CLAMP)


def e4m3fn_bytes(y):
    return np.clip(np.asarray(y, np.float64), -448.0, 448.0).astype(np.float32).astype(ml_dtypes.float8_e4m3fn).view(np.uint8)


def e4m3fn_values(b):
    return np.asarray(b, np.uint8).view(ml_dtypes.float8_e4m3fn).astype(np.float64)


def setup_inputs():
    d = draw0()
    x0 = np.asarray(d['encoder_out']).astype(np.float64)
    s = (np.max(np.abs(x0), axis=(0, 1), keepdims=True) / 448.0).astype(np.float32)
    out = {}
    for k, v in d.items():
        if k == 'encoder_out':
            out['encoder_out_bytes'] = e4m3fn_bytes(x0 / s.astype(np.float64))
            out['encoder_out_scale'] = s
        else:
            out[k] = v
    return out


def reference(encoder_out_bytes, encoder_out_scale, predictor_out, W_enc_words, W_enc_scales, b_enc, W_pred_words, W_pred_scales, b_pred, W_out_words, W_out_scales, b_out):
    return core(e4m3fn_values(encoder_out_bytes) * encoder_out_scale.astype(np.float64), predictor_out, W_enc_words, W_enc_scales, b_enc, W_pred_words, W_pred_scales, b_pred, W_out_words, W_out_scales, b_out)

@@ -1,0 +1,248 @@
+from contextlib import ExitStack
+
+import concourse.mybir as mybir
+from concourse.masks import make_identity
+
+F32 = mybir.dt.float32
+BF16 = mybir.dt.bfloat16
+I32 = mybir.dt.int32
+U32 = mybir.dt.uint32
+U8 = mybir.dt.uint8
+FP8 = mybir.dt.float8_e4m3fn
+FP8X4 = mybir.dt.float8_e4m3fn_x4
+FP4X4 = mybir.dt.float4_e2m1fn_x4
+ADD = mybir.AluOpType.add
+MULT = mybir.AluOpType.mult
+MIN = mybir.AluOpType.min
+MAX = mybir.AluOpType.max
+TANH = mybir.ActivationFunctionType.Tanh
+
+P = 128
+B, T, U, K, V = 4, 128, 32, 512, 128
+LIM = 15.0
+FLOPS = 2 * K * (B * T * K + B * U * K + B * T * U * V)
+
+
+def tile_jointnetwork_t_w4_kernel(tc, enc_bytes, enc_scale, pred, w_enc, s_enc, b_enc, w_pred, s_pred, b_pred, w_out, s_out, b_out, out):
+    nc = tc.nc
+    with ExitStack() as ctx:
+        keep = ctx.enter_context(tc.tile_pool(name="keep", bufs=1))
+        head = ctx.enter_context(tc.tile_pool(name="head", bufs=2))
+        sums = ctx.enter_context(tc.tile_pool(name="sums", bufs=3))
+        joints = ctx.enter_context(tc.tile_pool(name="joints", bufs=3))
+        results = ctx.enter_context(tc.tile_pool(name="results", bufs=4))
+        copies = ctx.enter_context(tc.tile_pool(name="copies", bufs=16))
+        psum = ctx.enter_context(tc.psum_pool(name="psum", bufs=8))
+        ctx.enter_context(tc.manual_schedule())
+
+        dummy = keep.tile([P, 1], F32, name="dummy")
+        nc.vector.memset(dummy[:], 0.0)
+        dummy_o = keep.tile([P, 1], F32, name="dummy_o")
+        nc.scalar.activation(out=dummy_o[:], in_=dummy[:], func=TANH)
+
+        stage_s = keep.tile([P, 2 * K + V], U8, name="stage_s", align_bytes=64)
+        nc.vector.memset(stage_s[:].bitcast(I32), 0)
+        ident = keep.tile([P, P], F32, name="ident")
+        make_identity(nc, ident[:])
+
+        scale_bc = keep.tile([P, K], F32, name="scale_bc")
+        nc.scalar.dma_start(out=scale_bc[:], in_=enc_scale.rearrange("a b k -> (a b k)").partition_broadcast(P))
+        codes_in = keep.tile([P, B, K], U8, name="codes_in")
+        nc.sync.dma_start(out=codes_in[:, 0, :], in_=enc_bytes[0])
+        pred_in = keep.tile([P, K], BF16, name="pred_in")
+        nc.scalar.dma_start(out=pred_in[:], in_=pred.rearrange("b u k -> (b u) k"))
+        wp_raw = keep.tile([P, 2 * K], U8, name="wp_raw", align_bytes=64)
+        nc.sync.dma_start(out=wp_raw[:], in_=w_pred[0])
+        we_raw = keep.tile([P, 2 * K], U8, name="we_raw", align_bytes=64)
+        nc.sync.dma_start(out=we_raw[:], in_=w_enc[0])
+        bias_e = keep.tile([P, 4], BF16, name="bias_e")
+        nc.scalar.dma_start(out=bias_e[:], in_=b_enc.rearrange("(p j) -> p j", j=4))
+        bias_p = keep.tile([P, 4], BF16, name="bias_p")
+        nc.scalar.dma_start(out=bias_p[:], in_=b_pred.rearrange("(p j) -> p j", j=4))
+        for src, lo, n in ((s_pred, K, K), (s_enc, 0, K), (s_out, 2 * K, V)):
+            for r in range(4):
+                nc.sync.dma_start(out=stage_s[r:P:32, lo:lo + n].bitcast(I32), in_=src[0].rearrange("(q r) n -> r q n", r=4)[r].bitcast(I32))
+        nc.sync.dma_start(out=codes_in[:, 1:B, :], in_=enc_bytes[1:B].rearrange("b t k -> t b k"))
+        wo = keep.tile([P, 2 * V], U8, name="wo", align_bytes=64)
+        nc.sync.dma_start(out=wo[:], in_=w_out[0])
+        bias_o = keep.tile([P, V], BF16, name="bias_o")
+        nc.scalar.dma_start(out=bias_o[:], in_=b_out.partition_broadcast(P))
+
+        wp = keep.tile([P, 2 * K], U8, name="wp", align_bytes=64)
+        we = keep.tile([P, 2 * K], U8, name="we", align_bytes=64)
+        sp = keep.tile([P, K], U8, name="sp", align_bytes=64)
+        se = keep.tile([P, K], U8, name="se", align_bytes=64)
+        so = keep.tile([P, V], U8, name="so", align_bytes=64)
+
+        def permute_words(dst, src):
+            nc.vector.tensor_copy(out=dst[:].rearrange("p (j m c) -> p j m c", j=4, c=2), in_=src[:].rearrange("p (m j c) -> p j m c", j=4, c=2))
+
+        def permute_scales(dst, lo):
+            nc.vector.tensor_copy(out=dst[:].rearrange("p (j m) -> p j m", j=4), in_=stage_s[:, lo:lo + K].rearrange("p (m j) -> p j m", j=4))
+
+        def turn(rows):
+            words = rows.bitcast(F32)
+            xt = psum.tile([P, 2, P], F32, name="xt", tag="bank")
+            for u in range(2):
+                nc.tensor.transpose(xt[:, u, :], words[:, u:2 * P:2], ident[:])
+            grouped = head.tile([P, P, 4], BF16, name="grouped", align_bytes=64)
+            nc.scalar.copy(out=grouped[:].rearrange("p r j -> p (r j)").bitcast(F32).rearrange("p (r u) -> p r u", u=2), in_=xt[:].rearrange("p u r -> p r u"))
+            return grouped
+
+        def quant(grouped):
+            q = head.tile([P, P], U32, name="q", align_bytes=64)
+            qs = head.tile([P, P], U8, name="qs", align_bytes=64)
+            nc.vector.quantize_mx(out=q[:].bitcast(FP8X4), scales=qs[:], in_=grouped[:].rearrange("p r j -> p (r j)"))
+            return q, qs
+
+        def project(w, s, q, qs):
+            acc = psum.tile([P, 4, P], F32, name="acc", tag="bank")
+            for j in range(4):
+                nc.tensor.matmul_mx(out=acc[:, j, :], lhsT=w[:, 2 * P * j:2 * P * (j + 1)].bitcast(FP4X4), lhsT_scale=s[:, P * j:P * (j + 1)], rhs=q[:].bitcast(FP8X4), rhs_scale=qs[:], start=True, stop=True)
+            return acc
+
+        g_pred = turn(pred_in[:])
+        permute_words(wp, wp_raw)
+        bias = keep.tile([P, 4], F32, name="bias")
+        x_enc = keep.tile([P, B, K], BF16, name="x_enc")
+
+        def widen(b):
+            nc.vector.tensor_tensor(out=x_enc[:, b, :], in0=codes_in[:, b, :].bitcast(FP8), in1=scale_bc[:], op=MULT)
+
+        widen(0)
+        nc.vector.tensor_tensor(out=bias[:], in0=bias_e[:], in1=bias_p[:], op=ADD)
+        q_pred = quant(g_pred)
+        g_enc = turn(x_enc[:, 0, :])
+        permute_words(we, we_raw)
+        permute_scales(sp, K)
+        acc = project(wp, sp, *q_pred)
+        q_enc = quant(g_enc)
+        permute_scales(se, 0)
+        predT = keep.tile([P, 4, P], F32, name="predT")
+        nc.vector.tensor_tensor(out=predT[:], in0=acc[:], in1=bias[:].unsqueeze(2).to_broadcast([P, 4, P]), op=ADD)
+        encT = keep.tile([P, 2, 4, P], F32, name="encT")
+        acc = project(we, se, *q_enc)
+        nc.scalar.copy(out=encT[:, 0], in_=acc[:])
+
+        back = psum.tile([P, 4, P], F32, name="back", tag="bank")
+        for j in range(4):
+            nc.tensor.transpose(back[:, j, :], predT[:, j, :], ident[:])
+        pred_rows = keep.tile([P, K], F32, name="pred_rows")
+        nc.scalar.copy(out=pred_rows[:], in_=back[:].rearrange("p j m -> p (j m)"))
+        scratch = out[B - 1, 0:16].rearrange("t u v -> (t u v)")
+        nc.sync.dma_start(out=scratch.rearrange("(r k) -> r k", k=K), in_=pred_rows[:])
+
+        nc.vector.tensor_copy(out=so[:], in_=stage_s[:, 2 * K:])
+        encR = keep.tile([P, 2, K], F32, name="encR")
+        for b in range(1, B):
+            widen(b)
+            g = turn(x_enc[:, b, :])
+            q, qs = quant(g)
+            if b < 2:
+                acc = project(we, se, q, qs)
+                nc.scalar.copy(out=encT[:, b], in_=acc[:])
+            else:
+                acc = psum.tile([P, K], F32, name="racc", tag="bank")
+                nc.tensor.matmul_mx(out=acc[:], lhsT=q[:].bitcast(FP8X4), lhsT_scale=qs[:], rhs=we[:].bitcast(FP4X4), rhs_scale=se[:], start=True, stop=True)
+                nc.scalar.copy(out=encR[:, b - 2, :], in_=acc[:])
+
+        shape = [(4, 0)] * 3 + [(2, 2)] * 23 + [(1, 3)] * 6
+        v_next, t_next = 0, 2 * U
+        steps = []
+        for nv, nt in shape:
+            steps.append((list(range(v_next, v_next + nv)), list(range(t_next, t_next + nt))))
+            v_next += nv
+            t_next += nt
+        n_steps = len(steps)
+        G = 2
+        copy_t = {}
+
+        def load_copies(i):
+            g = 2 * U + G * i
+            if g < B * U:
+                copy_t[i] = copies.tile([P, G, K], F32, name="copy")
+                nc.sync.dma_start(out=copy_t[i][:].rearrange("p g k -> p (g k)"), in_=scratch[g * K:(g + G) * K].partition_broadcast(P))
+
+        sum_t, bank_t, joint_t, code_t, acc_t, res_t = {}, {}, {}, {}, {}, {}
+
+        def adds(s, half):
+            vs = steps[s][0]
+            if half == 0 and vs:
+                sum_t[s] = sums.tile([P, 4, len(vs) * P], F32, name="sum", tag="sum%d" % len(vs))
+            k = (len(vs) + 1) // 2
+            for i, un in enumerate(vs):
+                if (i < k) == (half == 0):
+                    for j in range(4):
+                        nc.vector.tensor_scalar(out=sum_t[s][:, j, i * P:(i + 1) * P], in0=encT[:, un // U, j, :], scalar1=predT[:, j, un:un + 1], scalar2=None, op0=ADD)
+
+        def tensor_sums(s):
+            bank_t[s] = []
+            for un in steps[s][1]:
+                bank = psum.tile([P, 4, P], F32, name="tsum", tag="bank")
+                bank_t[s].append(bank)
+                i, g = divmod(un - 2 * U, G)
+                for j in range(4):
+                    cols = slice(j * P, (j + 1) * P)
+                    nc.tensor.matmul(bank[:, j, :], lhsT=encR[:, un // U - 2, cols], rhs=ident[:], start=True, stop=False, is_transpose=True)
+                    nc.tensor.matmul(bank[:, j, :], lhsT=copy_t[i][:, g, cols], rhs=ident[:], start=False, stop=True, is_transpose=True)
+
+        def tanh(s):
+            vs, ts = steps[s]
+            joint = joints.tile([P, 4 * P, 4], BF16, name="joint", align_bytes=64)
+            joint_t[s] = joint
+            if vs:
+                nc.scalar.activation(out=joint[:, 0:len(vs) * P, :].rearrange("p (c i) j -> p c j i", i=4), in_=sum_t[s][:].rearrange("p j (c i) -> p c j i", i=4), func=TANH)
+            for i, bank in enumerate(bank_t[s]):
+                r = (len(vs) + i) * P
+                nc.scalar.activation(out=joint[:, r:r + P, :], in_=bank[:].rearrange("p j n -> p n j"), func=TANH)
+
+        def quantize(c):
+            q = joints.tile([P, 4 * P], U32, name="jq", align_bytes=64)
+            qs = joints.tile([P, 4 * P], U8, name="jqs", align_bytes=64)
+            nc.vector.quantize_mx(out=q[:].bitcast(FP8X4), scales=qs[:], in_=joint_t[c][:].rearrange("p n j -> p (n j)"))
+            code_t[c] = (q, qs)
+
+        def multiply(c):
+            q, qs = code_t[c]
+            acc_t[c] = psum.tile([P, 4, V], F32, name="oacc", tag="bank")
+            for u in range(4):
+                nc.tensor.matmul_mx(out=acc_t[c][:, u, :], lhsT=q[:, u * P:(u + 1) * P].bitcast(FP8X4), lhsT_scale=qs[:, u * P:(u + 1) * P], rhs=wo[:].bitcast(FP4X4), rhs_scale=so[:], start=True, stop=True)
+
+        def add_bias(c):
+            res_t[c] = results.tile([P, 4, V], F32, name="res")
+            nc.vector.tensor_tensor(out=res_t[c][:], in0=acc_t[c][:], in1=bias_o[:].unsqueeze(1).to_broadcast([P, 4, V]), op=ADD)
+
+        def clip_store(c):
+            nc.vector.tensor_scalar(out=res_t[c][:], in0=res_t[c][:], scalar1=LIM, scalar2=-LIM, op0=MIN, op1=MAX)
+            col = 0
+            for units in steps[c]:
+                while units:
+                    n = 1
+                    while n < len(units) and units[n] // U == units[0] // U:
+                        n += 1
+                    b, u0 = divmod(units[0], U)
+                    nc.sync.dma_start(out=out[b, :, u0:u0 + n, :], in_=res_t[c][:, col:col + n, :])
+                    col += n
+                    units = units[n:]
+
+        for i in range(14):
+            load_copies(i)
+        adds(0, 0)
+        adds(0, 1)
+        tensor_sums(0)
+        for s in range(n_steps + 2):
+            if s < n_steps:
+                tanh(s)
+            if s + 1 < n_steps:
+                adds(s + 1, 0)
+                tensor_sums(s + 1)
+            if 1 <= s <= n_steps:
+                quantize(s - 1)
+                multiply(s - 1)
+            if s >= 2:
+                add_bias(s - 2)
+            if s + 1 < n_steps:
+                adds(s + 1, 1)
+            load_copies(14 + s)
+            if s >= 2:
+                clip_store(s - 2)

@@ -31,62 +31,78 @@ def tile_jointnetwork_t_w4_kernel(tc, enc_bytes, enc_scale, pred, w_enc, s_enc, 
         sums = ctx.enter_context(tc.tile_pool(name="sums", bufs=3))
         joints = ctx.enter_context(tc.tile_pool(name="joints", bufs=3))
         results = ctx.enter_context(tc.tile_pool(name="results", bufs=4))
-        copies = ctx.enter_context(tc.tile_pool(name="copies", bufs=16))
+        copies = ctx.enter_context(tc.tile_pool(name="copies", bufs=9))
         psum = ctx.enter_context(tc.psum_pool(name="psum", bufs=8))
         ctx.enter_context(tc.manual_schedule())
+
+        scale_bc = keep.tile([P, K], F32, name="scale_bc")
+        pred_in = keep.tile([P, K], BF16, name="pred_in")
+        codes_in = keep.tile([P, B, K], U8, name="codes_in")
+        wp_raw = keep.tile([P, 2 * K], U8, name="wp_raw", align_bytes=64)
+        we_raw = keep.tile([P, 2 * K], U8, name="we_raw", align_bytes=64)
+        sp_raw = keep.tile([P, K], U8, name="sp_raw", align_bytes=64)
+        se_raw = keep.tile([P, K], U8, name="se_raw", align_bytes=64)
+        wo = keep.tile([P, 2 * V], U8, name="wo", align_bytes=64)
+        so = keep.tile([P, V], U8, name="so", align_bytes=64)
+        bias_e = keep.tile([P, 4], BF16, name="bias_e")
+        bias_p = keep.tile([P, 4], BF16, name="bias_p")
+        bias_o = keep.tile([P, V], BF16, name="bias_o")
+
+        def load_scales(dst, src, n):
+            rows = src[0].rearrange("(q r) n -> r q n", r=4).bitcast(I32)
+            for r in range(4):
+                nc.sync.dma_start(out=dst[r:P:4, :].bitcast(I32), in_=rows[r].unsqueeze(1).to_broadcast([4, 8, n // 4]))
+
+        nc.gpsimd.dma_start(out=pred_in[:], in_=pred.rearrange("b u k -> (b u) k"))
+        nc.scalar.dma_start(out=scale_bc[:], in_=enc_scale.rearrange("a b k -> (a b k)").partition_broadcast(P))
+        nc.sync.dma_start(out=codes_in[:], in_=enc_bytes.rearrange("b t k -> t b k"))
+        nc.sync.dma_start(out=wp_raw[:], in_=w_pred[0])
+        load_scales(sp_raw, s_pred, K)
+        nc.sync.dma_start(out=we_raw[:], in_=w_enc[0])
+        load_scales(se_raw, s_enc, K)
+        nc.gpsimd.dma_start(out=bias_e[:], in_=b_enc.rearrange("(p j) -> p j", j=4))
+        nc.gpsimd.dma_start(out=bias_p[:], in_=b_pred.rearrange("(p j) -> p j", j=4))
+        nc.sync.dma_start(out=wo[:], in_=w_out[0])
+        load_scales(so, s_out, V)
 
         dummy = keep.tile([P, 1], F32, name="dummy")
         nc.vector.memset(dummy[:], 0.0)
         dummy_o = keep.tile([P, 1], F32, name="dummy_o")
         nc.scalar.activation(out=dummy_o[:], in_=dummy[:], func=TANH)
-
-        stage_s = keep.tile([P, 2 * K + V], U8, name="stage_s", align_bytes=64)
-        nc.vector.memset(stage_s[:].bitcast(I32), 0)
         ident = keep.tile([P, P], F32, name="ident")
         make_identity(nc, ident[:])
-
-        scale_bc = keep.tile([P, K], F32, name="scale_bc")
-        nc.scalar.dma_start(out=scale_bc[:], in_=enc_scale.rearrange("a b k -> (a b k)").partition_broadcast(P))
-        codes_in = keep.tile([P, B, K], U8, name="codes_in")
-        nc.sync.dma_start(out=codes_in[:, 0, :], in_=enc_bytes[0])
-        pred_in = keep.tile([P, K], BF16, name="pred_in")
-        nc.scalar.dma_start(out=pred_in[:], in_=pred.rearrange("b u k -> (b u) k"))
-        wp_raw = keep.tile([P, 2 * K], U8, name="wp_raw", align_bytes=64)
-        nc.sync.dma_start(out=wp_raw[:], in_=w_pred[0])
-        we_raw = keep.tile([P, 2 * K], U8, name="we_raw", align_bytes=64)
-        nc.sync.dma_start(out=we_raw[:], in_=w_enc[0])
-        bias_e = keep.tile([P, 4], BF16, name="bias_e")
-        nc.scalar.dma_start(out=bias_e[:], in_=b_enc.rearrange("(p j) -> p j", j=4))
-        bias_p = keep.tile([P, 4], BF16, name="bias_p")
-        nc.scalar.dma_start(out=bias_p[:], in_=b_pred.rearrange("(p j) -> p j", j=4))
-        for src, lo, n in ((s_pred, K, K), (s_enc, 0, K), (s_out, 2 * K, V)):
-            for r in range(4):
-                nc.sync.dma_start(out=stage_s[r:P:32, lo:lo + n].bitcast(I32), in_=src[0].rearrange("(q r) n -> r q n", r=4)[r].bitcast(I32))
-        nc.sync.dma_start(out=codes_in[:, 1:B, :], in_=enc_bytes[1:B].rearrange("b t k -> t b k"))
-        wo = keep.tile([P, 2 * V], U8, name="wo", align_bytes=64)
-        nc.sync.dma_start(out=wo[:], in_=w_out[0])
-        bias_o = keep.tile([P, V], BF16, name="bias_o")
-        nc.scalar.dma_start(out=bias_o[:], in_=b_out.partition_broadcast(P))
+        nc.gpsimd.dma_start(out=bias_o[:], in_=b_out.partition_broadcast(P))
 
         wp = keep.tile([P, 2 * K], U8, name="wp", align_bytes=64)
         we = keep.tile([P, 2 * K], U8, name="we", align_bytes=64)
         sp = keep.tile([P, K], U8, name="sp", align_bytes=64)
         se = keep.tile([P, K], U8, name="se", align_bytes=64)
-        so = keep.tile([P, V], U8, name="so", align_bytes=64)
+        bias = keep.tile([P, 4], F32, name="bias")
+        x_enc = keep.tile([P, B, K], BF16, name="x_enc")
+        predT = keep.tile([P, 4, P], F32, name="predT")
+        encT = keep.tile([P, 2, 4, P], F32, name="encT")
+        encR = keep.tile([P, 2, K], F32, name="encR")
+        pred_rows = keep.tile([P, K], F32, name="pred_rows")
 
         def permute_words(dst, src):
             nc.vector.tensor_copy(out=dst[:].rearrange("p (j m c) -> p j m c", j=4, c=2), in_=src[:].rearrange("p (m j c) -> p j m c", j=4, c=2))
 
-        def permute_scales(dst, lo):
-            nc.vector.tensor_copy(out=dst[:].rearrange("p (j m) -> p j m", j=4), in_=stage_s[:, lo:lo + K].rearrange("p (m j) -> p j m", j=4))
+        def permute_scales(dst, src):
+            nc.vector.tensor_copy(out=dst[:].rearrange("p (j m) -> p j m", j=4), in_=src[:].rearrange("p (m j) -> p j m", j=4))
+
+        def widen(b):
+            nc.vector.tensor_tensor(out=x_enc[:, b, :], in0=codes_in[:, b, :].bitcast(FP8), in1=scale_bc[:], op=MULT)
 
         def turn(rows):
             words = rows.bitcast(F32)
             xt = psum.tile([P, 2, P], F32, name="xt", tag="bank")
             for u in range(2):
                 nc.tensor.transpose(xt[:, u, :], words[:, u:2 * P:2], ident[:])
+            return xt
+
+        def group(copy, xt):
             grouped = head.tile([P, P, 4], BF16, name="grouped", align_bytes=64)
-            nc.scalar.copy(out=grouped[:].rearrange("p r j -> p (r j)").bitcast(F32).rearrange("p (r u) -> p r u", u=2), in_=xt[:].rearrange("p u r -> p r u"))
+            copy(out=grouped[:].rearrange("p r j -> p (r j)").bitcast(F32).rearrange("p (r u) -> p r u", u=2), in_=xt[:].rearrange("p u r -> p r u"))
             return grouped
 
         def quant(grouped):
@@ -101,67 +117,75 @@ def tile_jointnetwork_t_w4_kernel(tc, enc_bytes, enc_scale, pred, w_enc, s_enc, 
                 nc.tensor.matmul_mx(out=acc[:, j, :], lhsT=w[:, 2 * P * j:2 * P * (j + 1)].bitcast(FP4X4), lhsT_scale=s[:, P * j:P * (j + 1)], rhs=q[:].bitcast(FP8X4), rhs_scale=qs[:], start=True, stop=True)
             return acc
 
-        g_pred = turn(pred_in[:])
+        def project_rows(q, qs):
+            acc = psum.tile([P, K], F32, name="racc", tag="bank")
+            nc.tensor.matmul_mx(out=acc[:], lhsT=q[:].bitcast(FP8X4), lhsT_scale=qs[:], rhs=we[:].bitcast(FP4X4), rhs_scale=se[:], start=True, stop=True)
+            return acc
+
+        xt = turn(pred_in[:])
+        g_pred = group(nc.scalar.copy, xt)
         permute_words(wp, wp_raw)
-        bias = keep.tile([P, 4], F32, name="bias")
-        x_enc = keep.tile([P, B, K], BF16, name="x_enc")
-
-        def widen(b):
-            nc.vector.tensor_tensor(out=x_enc[:, b, :], in0=codes_in[:, b, :].bitcast(FP8), in1=scale_bc[:], op=MULT)
-
         widen(0)
-        nc.vector.tensor_tensor(out=bias[:], in0=bias_e[:], in1=bias_p[:], op=ADD)
+        permute_scales(sp, sp_raw)
         q_pred = quant(g_pred)
-        g_enc = turn(x_enc[:, 0, :])
+        xt = turn(x_enc[:, 0, :])
+        g_enc = group(nc.scalar.copy, xt)
+        acc_p = project(wp, sp, *q_pred)
+        nc.vector.tensor_tensor(out=bias[:], in0=bias_e[:], in1=bias_p[:], op=ADD)
         permute_words(we, we_raw)
-        permute_scales(sp, K)
-        acc = project(wp, sp, *q_pred)
+        permute_scales(se, se_raw)
         q_enc = quant(g_enc)
-        permute_scales(se, 0)
-        predT = keep.tile([P, 4, P], F32, name="predT")
-        nc.vector.tensor_tensor(out=predT[:], in0=acc[:], in1=bias[:].unsqueeze(2).to_broadcast([P, 4, P]), op=ADD)
-        encT = keep.tile([P, 2, 4, P], F32, name="encT")
+        nc.vector.tensor_tensor(out=predT[:], in0=acc_p[:], in1=bias[:].unsqueeze(2).to_broadcast([P, 4, P]), op=ADD)
         acc = project(we, se, *q_enc)
         nc.scalar.copy(out=encT[:, 0], in_=acc[:])
 
         back = psum.tile([P, 4, P], F32, name="back", tag="bank")
         for j in range(4):
             nc.tensor.transpose(back[:, j, :], predT[:, j, :], ident[:])
-        pred_rows = keep.tile([P, K], F32, name="pred_rows")
         nc.scalar.copy(out=pred_rows[:], in_=back[:].rearrange("p j m -> p (j m)"))
-        scratch = out[B - 1, 0:16].rearrange("t u v -> (t u v)")
-        nc.sync.dma_start(out=scratch.rearrange("(r k) -> r k", k=K), in_=pred_rows[:])
+        R = 4
+        scratch = out[B - 1, :, 3 * U // 4:U, :].rearrange("(r a) u v -> r a (u v)", r=R)
+        for r in range(R):
+            nc.sync.dma_start(out=scratch[r].rearrange("a (e k) -> a e k", e=2), in_=pred_rows[2 * U:4 * U, :])
 
-        nc.vector.tensor_copy(out=so[:], in_=stage_s[:, 2 * K:])
-        encR = keep.tile([P, 2, K], F32, name="encR")
-        for b in range(1, B):
-            widen(b)
-            g = turn(x_enc[:, b, :])
-            q, qs = quant(g)
-            if b < 2:
-                acc = project(we, se, q, qs)
-                nc.scalar.copy(out=encT[:, b], in_=acc[:])
+        prep = {}
+
+        def prepare(b, stage, copy):
+            if stage == 0:
+                widen(b)
+                prep[b] = turn(x_enc[:, b, :])
+            elif stage == 1:
+                prep[b] = group(copy, prep[b])
+            elif stage == 2:
+                q = quant(prep[b])
+                prep[b] = project(we, se, *q) if b < 2 else project_rows(*q)
             else:
-                acc = psum.tile([P, K], F32, name="racc", tag="bank")
-                nc.tensor.matmul_mx(out=acc[:], lhsT=q[:].bitcast(FP8X4), lhsT_scale=qs[:], rhs=we[:].bitcast(FP4X4), rhs_scale=se[:], start=True, stop=True)
-                nc.scalar.copy(out=encR[:, b - 2, :], in_=acc[:])
+                copy(out=encT[:, b] if b < 2 else encR[:, b - 2, :], in_=prep[b][:])
 
-        shape = [(4, 0)] * 3 + [(2, 2)] * 23 + [(1, 3)] * 6
+        shape = [(1, 0), (1, 0), (2, 0), (4, 0), (4, 0), (4, 0)]
+        for i in range(7):
+            shape += [(2, 2)] * 3 + [(1, 3)] if i < 6 else [(2, 2)] * 2
+        shape += [(1, 3), (1, 1), (0, 1), (0, 1)]
         v_next, t_next = 0, 2 * U
         steps = []
         for nv, nt in shape:
             steps.append((list(range(v_next, v_next + nv)), list(range(t_next, t_next + nt))))
             v_next += nv
             t_next += nt
+        assert v_next == 2 * U and t_next == 4 * U, (v_next, t_next)
         n_steps = len(steps)
-        G = 2
+        groups = [2] * U
+        starts = [sum(groups[:i]) for i in range(len(groups))]
+        where = {}
         copy_t = {}
 
         def load_copies(i):
-            g = 2 * U + G * i
-            if g < B * U:
-                copy_t[i] = copies.tile([P, G, K], F32, name="copy")
-                nc.sync.dma_start(out=copy_t[i][:].rearrange("p g k -> p (g k)"), in_=scratch[g * K:(g + G) * K].partition_broadcast(P))
+            if i < len(groups):
+                t = copies.tile([P, 2, K], F32, name="copy")
+                n = groups[i]
+                nc.sync.dma_start(out=t[:, 0:n, :].rearrange("p g k -> p (g k)"), in_=scratch[:, i, :].unsqueeze(1).to_broadcast([R, P // R, n * K]))
+                for g in range(n):
+                    where[2 * U + starts[i] + g] = (t, g, i if g == n - 1 else -1)
 
         sum_t, bank_t, joint_t, code_t, acc_t, res_t = {}, {}, {}, {}, {}, {}
 
@@ -180,15 +204,18 @@ def tile_jointnetwork_t_w4_kernel(tc, enc_bytes, enc_scale, pred, w_enc, s_enc, 
             for un in steps[s][1]:
                 bank = psum.tile([P, 4, P], F32, name="tsum", tag="bank")
                 bank_t[s].append(bank)
-                i, g = divmod(un - 2 * U, G)
+                t, g, last = where[un]
                 for j in range(4):
                     cols = slice(j * P, (j + 1) * P)
                     nc.tensor.matmul(bank[:, j, :], lhsT=encR[:, un // U - 2, cols], rhs=ident[:], start=True, stop=False, is_transpose=True)
-                    nc.tensor.matmul(bank[:, j, :], lhsT=copy_t[i][:, g, cols], rhs=ident[:], start=False, stop=True, is_transpose=True)
+                    nc.tensor.matmul(bank[:, j, :], lhsT=t[:, g, cols], rhs=ident[:], start=False, stop=True, is_transpose=True)
+                if last >= 0:
+                    load_copies(last + 5)
 
         def tanh(s):
             vs, ts = steps[s]
-            joint = joints.tile([P, 4 * P, 4], BF16, name="joint", align_bytes=64)
+            n = len(vs) + len(ts)
+            joint = joints.tile([P, n * P, 4], BF16, name="joint", tag="joint%d" % n, align_bytes=64)
             joint_t[s] = joint
             if vs:
                 nc.scalar.activation(out=joint[:, 0:len(vs) * P, :].rearrange("p (c i) j -> p c j i", i=4), in_=sum_t[s][:].rearrange("p j (c i) -> p c j i", i=4), func=TANH)
@@ -196,45 +223,51 @@ def tile_jointnetwork_t_w4_kernel(tc, enc_bytes, enc_scale, pred, w_enc, s_enc, 
                 r = (len(vs) + i) * P
                 nc.scalar.activation(out=joint[:, r:r + P, :], in_=bank[:].rearrange("p j n -> p n j"), func=TANH)
 
-        def quantize(c):
-            q = joints.tile([P, 4 * P], U32, name="jq", align_bytes=64)
-            qs = joints.tile([P, 4 * P], U8, name="jqs", align_bytes=64)
-            nc.vector.quantize_mx(out=q[:].bitcast(FP8X4), scales=qs[:], in_=joint_t[c][:].rearrange("p n j -> p (n j)"))
-            code_t[c] = (q, qs)
+        def quantize(s):
+            n = sum(len(x) for x in steps[s])
+            q = joints.tile([P, n * P], U32, name="jq", tag="jq%d" % n, align_bytes=64)
+            qs = joints.tile([P, n * P], U8, name="jqs", tag="jqs%d" % n, align_bytes=64)
+            nc.vector.quantize_mx(out=q[:].bitcast(FP8X4), scales=qs[:], in_=joint_t[s][:].rearrange("p n j -> p (n j)"))
+            code_t[s] = (q, qs, n)
 
-        def multiply(c):
-            q, qs = code_t[c]
-            acc_t[c] = psum.tile([P, 4, V], F32, name="oacc", tag="bank")
-            for u in range(4):
-                nc.tensor.matmul_mx(out=acc_t[c][:, u, :], lhsT=q[:, u * P:(u + 1) * P].bitcast(FP8X4), lhsT_scale=qs[:, u * P:(u + 1) * P], rhs=wo[:].bitcast(FP4X4), rhs_scale=so[:], start=True, stop=True)
+        def multiply(s):
+            q, qs, n = code_t[s]
+            acc_t[s] = psum.tile([P, n, V], F32, name="oacc", tag="bank")
+            for u in range(n):
+                nc.tensor.matmul_mx(out=acc_t[s][:, u, :], lhsT=q[:, u * P:(u + 1) * P].bitcast(FP8X4), lhsT_scale=qs[:, u * P:(u + 1) * P], rhs=wo[:].bitcast(FP4X4), rhs_scale=so[:], start=True, stop=True)
 
-        def add_bias(c):
-            res_t[c] = results.tile([P, 4, V], F32, name="res")
-            nc.vector.tensor_tensor(out=res_t[c][:], in0=acc_t[c][:], in1=bias_o[:].unsqueeze(1).to_broadcast([P, 4, V]), op=ADD)
+        def add_bias(s):
+            n = code_t[s][2]
+            res_t[s] = results.tile([P, 4, V], F32, name="res")
+            nc.vector.tensor_tensor(out=res_t[s][:, 0:n, :], in0=acc_t[s][:], in1=bias_o[:].unsqueeze(1).to_broadcast([P, n, V]), op=ADD)
 
-        def clip_store(c):
-            nc.vector.tensor_scalar(out=res_t[c][:], in0=res_t[c][:], scalar1=LIM, scalar2=-LIM, op0=MIN, op1=MAX)
+        def clip_store(s):
+            n = code_t[s][2]
+            nc.vector.tensor_scalar(out=res_t[s][:, 0:n, :], in0=res_t[s][:, 0:n, :], scalar1=LIM, scalar2=-LIM, op0=MIN, op1=MAX)
             col = 0
-            for units in steps[c]:
+            for units in steps[s]:
                 while units:
                     n = 1
                     while n < len(units) and units[n] // U == units[0] // U:
                         n += 1
                     b, u0 = divmod(units[0], U)
-                    nc.sync.dma_start(out=out[b, :, u0:u0 + n, :], in_=res_t[c][:, col:col + n, :])
+                    nc.sync.dma_start(out=out[b, :, u0:u0 + n, :], in_=res_t[s][:, col:col + n, :])
                     col += n
                     units = units[n:]
 
-        for i in range(14):
+        work = {0: [(2, 0)], 1: [(2, 1)], 2: [(2, 2)], 3: [(2, 3)], 6: [(1, 0)], 7: [(1, 1)], 8: [(1, 2)], 9: [(1, 3)], 12: [(3, 0)], 13: [(3, 1)], 14: [(3, 2)], 15: [(3, 3)]}
+        for i in range(5):
             load_copies(i)
         adds(0, 0)
-        adds(0, 1)
         tensor_sums(0)
         for s in range(n_steps + 2):
             if s < n_steps:
                 tanh(s)
             if s + 1 < n_steps:
                 adds(s + 1, 0)
+            for b, stage in work.get(s, []):
+                prepare(b, stage, nc.scalar.copy if b == 2 else nc.vector.tensor_copy)
+            if s + 1 < n_steps:
                 tensor_sums(s + 1)
             if 1 <= s <= n_steps:
                 quantize(s - 1)
@@ -243,6 +276,5 @@ def tile_jointnetwork_t_w4_kernel(tc, enc_bytes, enc_scale, pred, w_enc, s_enc, 
                 add_bias(s - 2)
             if s + 1 < n_steps:
                 adds(s + 1, 1)
-            load_copies(14 + s)
             if s >= 2:
                 clip_store(s - 2)

@@ -31,7 +31,6 @@ def tile_jointnetwork_t_w4_kernel(tc, enc_bytes, enc_scale, pred, w_enc, s_enc, 
         sums = ctx.enter_context(tc.tile_pool(name="sums", bufs=3))
         joints = ctx.enter_context(tc.tile_pool(name="joints", bufs=3))
         results = ctx.enter_context(tc.tile_pool(name="results", bufs=4))
-        copies = ctx.enter_context(tc.tile_pool(name="copies", bufs=9))
         psum = ctx.enter_context(tc.psum_pool(name="psum", bufs=8))
         ctx.enter_context(tc.manual_schedule())
 
@@ -143,10 +142,21 @@ def tile_jointnetwork_t_w4_kernel(tc, enc_bytes, enc_scale, pred, w_enc, s_enc, 
         for j in range(4):
             nc.tensor.transpose(back[:, j, :], predT[:, j, :], ident[:])
         nc.scalar.copy(out=pred_rows[:], in_=back[:].rearrange("p j m -> p (j m)"))
-        R = 4
-        scratch = out[B - 1, :, 3 * U // 4:U, :].rearrange("(r a) u v -> r a (u v)", r=R)
-        for r in range(R):
-            nc.sync.dma_start(out=scratch[r].rearrange("a (e k) -> a e k", e=2), in_=pred_rows[2 * U:4 * U, :])
+        enc_scratch = out[B - 1, 0:32].rearrange("(c t) u v -> c t (u v)", c=2)
+        pred_scratch = out[B - 1, 32:40].rearrange("t u v -> (t u v)")
+        nc.sync.dma_start(out=pred_scratch.rearrange("(p k) -> p k", k=K), in_=pred_rows[2 * U:4 * U, :])
+        enc_rep = [keep.tile([P, 8 * K], F32, name="enc_rep%d" % c) for c in range(2)]
+        pred_rep = [keep.tile([P, 4 * K], F32, name="pred_rep%d" % c) for c in range(2)]
+
+        def load_pred_rep(c):
+            src = pred_scratch.rearrange("(c a k) -> c a k", c=2, a=8)[c]
+            nc.sync.dma_start(out=pred_rep[c][:], in_=src.unsqueeze(0).to_broadcast([16, 8, 4 * K]))
+
+        def load_enc_rep(c, lo, hi):
+            src = enc_scratch[c].rearrange("t n -> (t n)").rearrange("(a k) -> a k", a=16)
+            nc.sync.dma_start(out=enc_rep[c][:, lo * K:hi * K], in_=src[:, lo * K:hi * K].unsqueeze(1).to_broadcast([16, 8, (hi - lo) * K]))
+
+        load_pred_rep(0)
 
         prep = {}
 
@@ -161,6 +171,12 @@ def tile_jointnetwork_t_w4_kernel(tc, enc_bytes, enc_scale, pred, w_enc, s_enc, 
                 prep[b] = project(we, se, *q) if b < 2 else project_rows(*q)
             else:
                 copy(out=encT[:, b] if b < 2 else encR[:, b - 2, :], in_=prep[b][:])
+                if b >= 2:
+                    nc.sync.dma_start(out=enc_scratch[b - 2].rearrange("t n -> (t n)").rearrange("(p k) -> p k", k=K), in_=encR[:, b - 2, :])
+                    load_enc_rep(b - 2, 0, 2)
+                    load_enc_rep(b - 2, 2, 8)
+                    if b == 3:
+                        load_pred_rep(1)
 
         shape = [(1, 0), (1, 0), (2, 0), (4, 0), (4, 0), (4, 0)]
         for i in range(7):
@@ -174,19 +190,6 @@ def tile_jointnetwork_t_w4_kernel(tc, enc_bytes, enc_scale, pred, w_enc, s_enc, 
             t_next += nt
         assert v_next == 2 * U and t_next == 4 * U, (v_next, t_next)
         n_steps = len(steps)
-        groups = [2] * U
-        starts = [sum(groups[:i]) for i in range(len(groups))]
-        where = {}
-        copy_t = {}
-
-        def load_copies(i):
-            if i < len(groups):
-                t = copies.tile([P, 2, K], F32, name="copy")
-                n = groups[i]
-                nc.sync.dma_start(out=t[:, 0:n, :].rearrange("p g k -> p (g k)"), in_=scratch[:, i, :].unsqueeze(1).to_broadcast([R, P // R, n * K]))
-                for g in range(n):
-                    where[2 * U + starts[i] + g] = (t, g, i if g == n - 1 else -1)
-
         sum_t, bank_t, joint_t, code_t, acc_t, res_t = {}, {}, {}, {}, {}, {}
 
         def adds(s, half):
@@ -204,13 +207,11 @@ def tile_jointnetwork_t_w4_kernel(tc, enc_bytes, enc_scale, pred, w_enc, s_enc, 
             for un in steps[s][1]:
                 bank = psum.tile([P, 4, P], F32, name="tsum", tag="bank")
                 bank_t[s].append(bank)
-                t, g, last = where[un]
+                c, i = divmod(un - 2 * U, U)
+                tg, ug = divmod(i, 4)
                 for j in range(4):
-                    cols = slice(j * P, (j + 1) * P)
-                    nc.tensor.matmul(bank[:, j, :], lhsT=encR[:, un // U - 2, cols], rhs=ident[:], start=True, stop=False, is_transpose=True)
-                    nc.tensor.matmul(bank[:, j, :], lhsT=t[:, g, cols], rhs=ident[:], start=False, stop=True, is_transpose=True)
-                if last >= 0:
-                    load_copies(last + 5)
+                    nc.tensor.matmul(bank[:, j, :], lhsT=enc_rep[c][:, tg * K + j * P:tg * K + (j + 1) * P], rhs=ident[:], start=True, stop=False, is_transpose=True)
+                    nc.tensor.matmul(bank[:, j, :], lhsT=pred_rep[c][:, ug * K + j * P:ug * K + (j + 1) * P], rhs=ident[:], start=False, stop=True, is_transpose=True)
 
         def tanh(s):
             vs, ts = steps[s]
@@ -244,21 +245,29 @@ def tile_jointnetwork_t_w4_kernel(tc, enc_bytes, enc_scale, pred, w_enc, s_enc, 
         def clip_store(s):
             n = code_t[s][2]
             nc.vector.tensor_scalar(out=res_t[s][:, 0:n, :], in0=res_t[s][:, 0:n, :], scalar1=LIM, scalar2=-LIM, op0=MIN, op1=MAX)
+            vs, ts = steps[s]
             col = 0
-            for units in steps[s]:
-                while units:
-                    n = 1
-                    while n < len(units) and units[n] // U == units[0] // U:
-                        n += 1
-                    b, u0 = divmod(units[0], U)
-                    nc.sync.dma_start(out=out[b, :, u0:u0 + n, :], in_=res_t[s][:, col:col + n, :])
-                    col += n
-                    units = units[n:]
+            while vs or ts:
+                units = vs or ts
+                block = U if vs else 4
+                n = 1
+                while n < len(units) and units[n] // block == units[0] // block:
+                    n += 1
+                b, u0 = divmod(units[0], U)
+                if vs:
+                    dst = out[b, :, u0:u0 + n, :]
+                    vs = vs[n:]
+                else:
+                    tg, ug = divmod(u0, 4)
+                    dst = out[b].rearrange("(a g) (c h) v -> g a c h v", g=8, h=4)[tg][:, :, ug:ug + n, :]
+                    ts = ts[n:]
+                nc.sync.dma_start(out=dst, in_=res_t[s][:, col:col + n, :])
+                col += n
 
-        work = {0: [(2, 0)], 1: [(2, 1)], 2: [(2, 2)], 3: [(2, 3)], 6: [(1, 0)], 7: [(1, 1)], 8: [(1, 2)], 9: [(1, 3)], 12: [(3, 0)], 13: [(3, 1)], 14: [(3, 2)], 15: [(3, 3)]}
-        for i in range(5):
-            load_copies(i)
+        work = {0: [(2, 2)], 1: [(2, 3)], 6: [(1, 0)], 7: [(1, 1)], 8: [(1, 2)], 9: [(1, 3)], 12: [(3, 0)], 13: [(3, 1)], 14: [(3, 2)], 15: [(3, 3)]}
+        prepare(2, 0, None)
         adds(0, 0)
+        prepare(2, 1, nc.scalar.copy)
         tensor_sums(0)
         for s in range(n_steps + 2):
             if s < n_steps:

@@ -28,11 +28,14 @@ def tile_jointnetwork_t_w4_kernel(tc, enc_bytes, enc_scale, pred, w_enc, s_enc, 
     with ExitStack() as ctx:
         keep = ctx.enter_context(tc.tile_pool(name="keep", bufs=1))
         head = ctx.enter_context(tc.tile_pool(name="head", bufs=2))
-        sums = ctx.enter_context(tc.tile_pool(name="sums", bufs=3))
+        planes = ctx.enter_context(tc.tile_pool(name="planes", bufs=3))
         joints = ctx.enter_context(tc.tile_pool(name="joints", bufs=3))
         results = ctx.enter_context(tc.tile_pool(name="results", bufs=4))
         psum = ctx.enter_context(tc.psum_pool(name="psum", bufs=8))
         ctx.enter_context(tc.manual_schedule())
+
+        ident = keep.tile([P, P], F32, name="ident")
+        make_identity(nc, ident[:])
 
         scale_bc = keep.tile([P, K], F32, name="scale_bc")
         pred_in = keep.tile([P, K], BF16, name="pred_in")
@@ -52,15 +55,16 @@ def tile_jointnetwork_t_w4_kernel(tc, enc_bytes, enc_scale, pred, w_enc, s_enc, 
             for r in range(4):
                 nc.sync.dma_start(out=dst[r:P:4, :].bitcast(I32), in_=rows[r].unsqueeze(1).to_broadcast([4, 8, n // 4]))
 
-        nc.gpsimd.dma_start(out=pred_in[:], in_=pred.rearrange("b u k -> (b u) k"))
+        nc.scalar.dma_start(out=pred_in[:], in_=pred.rearrange("b u k -> (b u) k"))
         nc.scalar.dma_start(out=scale_bc[:], in_=enc_scale.rearrange("a b k -> (a b k)").partition_broadcast(P))
-        nc.sync.dma_start(out=codes_in[:], in_=enc_bytes.rearrange("b t k -> t b k"))
+        nc.sync.dma_start(out=codes_in[:, 0:B:3, :], in_=enc_bytes[0:B:3].rearrange("b t k -> t b k"))
         nc.sync.dma_start(out=wp_raw[:], in_=w_pred[0])
         load_scales(sp_raw, s_pred, K)
         nc.sync.dma_start(out=we_raw[:], in_=w_enc[0])
         load_scales(se_raw, s_enc, K)
         nc.gpsimd.dma_start(out=bias_e[:], in_=b_enc.rearrange("(p j) -> p j", j=4))
         nc.gpsimd.dma_start(out=bias_p[:], in_=b_pred.rearrange("(p j) -> p j", j=4))
+        nc.sync.dma_start(out=codes_in[:, 1:3, :], in_=enc_bytes[1:3].rearrange("b t k -> t b k"))
         nc.sync.dma_start(out=wo[:], in_=w_out[0])
         load_scales(so, s_out, V)
 
@@ -68,8 +72,6 @@ def tile_jointnetwork_t_w4_kernel(tc, enc_bytes, enc_scale, pred, w_enc, s_enc, 
         nc.vector.memset(dummy[:], 0.0)
         dummy_o = keep.tile([P, 1], F32, name="dummy_o")
         nc.scalar.activation(out=dummy_o[:], in_=dummy[:], func=TANH)
-        ident = keep.tile([P, P], F32, name="ident")
-        make_identity(nc, ident[:])
         nc.gpsimd.dma_start(out=bias_o[:], in_=b_out.partition_broadcast(P))
 
         wp = keep.tile([P, 2 * K], U8, name="wp", align_bytes=64)
@@ -79,8 +81,8 @@ def tile_jointnetwork_t_w4_kernel(tc, enc_bytes, enc_scale, pred, w_enc, s_enc, 
         bias = keep.tile([P, 4], F32, name="bias")
         x_enc = keep.tile([P, B, K], BF16, name="x_enc")
         predT = keep.tile([P, 4, P], F32, name="predT")
-        encT = keep.tile([P, 2, 4, P], F32, name="encT")
-        encR = keep.tile([P, 2, K], F32, name="encR")
+        encT = keep.tile([P, 3, 4, P], F32, name="encT")
+        encR = keep.tile([P, K], F32, name="encR")
         pred_rows = keep.tile([P, K], F32, name="pred_rows")
 
         def permute_words(dst, src):
@@ -123,8 +125,8 @@ def tile_jointnetwork_t_w4_kernel(tc, enc_bytes, enc_scale, pred, w_enc, s_enc, 
 
         xt = turn(pred_in[:])
         g_pred = group(nc.scalar.copy, xt)
-        permute_words(wp, wp_raw)
         widen(0)
+        permute_words(wp, wp_raw)
         permute_scales(sp, sp_raw)
         q_pred = quant(g_pred)
         xt = turn(x_enc[:, 0, :])
@@ -142,21 +144,21 @@ def tile_jointnetwork_t_w4_kernel(tc, enc_bytes, enc_scale, pred, w_enc, s_enc, 
         for j in range(4):
             nc.tensor.transpose(back[:, j, :], predT[:, j, :], ident[:])
         nc.scalar.copy(out=pred_rows[:], in_=back[:].rearrange("p j m -> p (j m)"))
-        enc_scratch = out[B - 1, 0:32].rearrange("(c t) u v -> c t (u v)", c=2)
-        pred_scratch = out[B - 1, 32:40].rearrange("t u v -> (t u v)")
-        nc.sync.dma_start(out=pred_scratch.rearrange("(p k) -> p k", k=K), in_=pred_rows[2 * U:4 * U, :])
-        enc_rep = [keep.tile([P, 8 * K], F32, name="enc_rep%d" % c) for c in range(2)]
-        pred_rep = [keep.tile([P, 4 * K], F32, name="pred_rep%d" % c) for c in range(2)]
+        enc_scratch = out[B - 1, 0:16].rearrange("t u v -> (t u v)")
+        pred_scratch = out[B - 1, 16:20].rearrange("t u v -> (t u v)")
+        nc.sync.dma_start(out=pred_scratch.rearrange("(p k) -> p k", k=K), in_=pred_rows[3 * U:4 * U, :])
+        enc_rep = keep.tile([P, 8 * K], F32, name="enc_rep")
+        pred_rep = keep.tile([P, 4 * K], F32, name="pred_rep")
 
-        def load_pred_rep(c):
-            src = pred_scratch.rearrange("(c a k) -> c a k", c=2, a=8)[c]
-            nc.sync.dma_start(out=pred_rep[c][:], in_=src.unsqueeze(0).to_broadcast([16, 8, 4 * K]))
+        def load_pred_rep(lo, hi):
+            src = pred_scratch.rearrange("(c n) -> c n", c=8)
+            nc.sync.dma_start(out=pred_rep[:, lo * K:hi * K], in_=src[:, lo * K:hi * K].unsqueeze(0).to_broadcast([16, 8, (hi - lo) * K]))
 
-        def load_enc_rep(c, lo, hi):
-            src = enc_scratch[c].rearrange("t n -> (t n)").rearrange("(a k) -> a k", a=16)
-            nc.sync.dma_start(out=enc_rep[c][:, lo * K:hi * K], in_=src[:, lo * K:hi * K].unsqueeze(1).to_broadcast([16, 8, (hi - lo) * K]))
+        def load_enc_rep(lo, hi):
+            src = enc_scratch.rearrange("(a n) -> a n", a=16)
+            nc.sync.dma_start(out=enc_rep[:, lo * K:hi * K], in_=src[:, lo * K:hi * K].unsqueeze(1).to_broadcast([16, 8, (hi - lo) * K]))
 
-        load_pred_rep(0)
+        load_pred_rep(0, 2)
 
         prep = {}
 
@@ -168,61 +170,56 @@ def tile_jointnetwork_t_w4_kernel(tc, enc_bytes, enc_scale, pred, w_enc, s_enc, 
                 prep[b] = group(copy, prep[b])
             elif stage == 2:
                 q = quant(prep[b])
-                prep[b] = project(we, se, *q) if b < 2 else project_rows(*q)
+                prep[b] = project(we, se, *q) if b < 3 else project_rows(*q)
+            elif b < 3:
+                copy(out=encT[:, b], in_=prep[b][:])
             else:
-                copy(out=encT[:, b] if b < 2 else encR[:, b - 2, :], in_=prep[b][:])
-                if b >= 2:
-                    nc.sync.dma_start(out=enc_scratch[b - 2].rearrange("t n -> (t n)").rearrange("(p k) -> p k", k=K), in_=encR[:, b - 2, :])
-                    load_enc_rep(b - 2, 0, 2)
-                    load_enc_rep(b - 2, 2, 8)
-                    if b == 3:
-                        load_pred_rep(1)
+                copy(out=encR[:], in_=prep[b][:])
+                nc.sync.dma_start(out=enc_scratch.rearrange("(p k) -> p k", k=K), in_=encR[:])
+                load_enc_rep(0, 1)
+                load_pred_rep(2, 4)
+                load_enc_rep(1, 8)
 
-        shape = [(1, 0), (1, 0), (2, 0), (4, 0), (4, 0), (4, 0)]
-        for i in range(7):
-            shape += [(2, 2)] * 3 + [(1, 3)] if i < 6 else [(2, 2)] * 2
-        shape += [(1, 3), (1, 1), (0, 1), (0, 1)]
-        v_next, t_next = 0, 2 * U
+        shape = [(1, 0), (1, 0), (2, 0), (4, 0), (4, 0)]
+        for i in range(28):
+            shape.append((2, 2) if i in (8, 16, 24) else (3, 1))
+        shape += [(1, 1), (1, 0), (1, 0)]
+        v_units = [(b, u) for b in range(3) for u in range(U)]
+        t_units = [(tg, ug) for tg in range(8) for ug in range(4)]
         steps = []
         for nv, nt in shape:
-            steps.append((list(range(v_next, v_next + nv)), list(range(t_next, t_next + nt))))
-            v_next += nv
-            t_next += nt
-        assert v_next == 2 * U and t_next == 4 * U, (v_next, t_next)
+            steps.append((v_units[:nv], t_units[:nt]))
+            v_units, t_units = v_units[nv:], t_units[nt:]
+        assert not v_units and not t_units, (len(v_units), len(t_units))
         n_steps = len(steps)
-        sum_t, bank_t, joint_t, code_t, acc_t, res_t = {}, {}, {}, {}, {}, {}
-
-        def adds(s, half):
-            vs = steps[s][0]
-            if half == 0 and vs:
-                sum_t[s] = sums.tile([P, 4, len(vs) * P], F32, name="sum", tag="sum%d" % len(vs))
-            k = (len(vs) + 1) // 2
-            for i, un in enumerate(vs):
-                if (i < k) == (half == 0):
-                    for j in range(4):
-                        nc.vector.tensor_scalar(out=sum_t[s][:, j, i * P:(i + 1) * P], in0=encT[:, un // U, j, :], scalar1=predT[:, j, un:un + 1], scalar2=None, op0=ADD)
+        bank_t, plane_t, joint_t, code_t, acc_t, res_t = {}, {}, {}, {}, {}, {}
 
         def tensor_sums(s):
             bank_t[s] = []
-            for un in steps[s][1]:
+            for tg, ug in steps[s][1]:
                 bank = psum.tile([P, 4, P], F32, name="tsum", tag="bank")
                 bank_t[s].append(bank)
-                c, i = divmod(un - 2 * U, U)
-                tg, ug = divmod(i, 4)
                 for j in range(4):
-                    nc.tensor.matmul(bank[:, j, :], lhsT=enc_rep[c][:, tg * K + j * P:tg * K + (j + 1) * P], rhs=ident[:], start=True, stop=False, is_transpose=True)
-                    nc.tensor.matmul(bank[:, j, :], lhsT=pred_rep[c][:, ug * K + j * P:ug * K + (j + 1) * P], rhs=ident[:], start=False, stop=True, is_transpose=True)
+                    nc.tensor.matmul(bank[:, j, :], lhsT=enc_rep[:, tg * K + j * P:tg * K + (j + 1) * P], rhs=ident[:], start=True, stop=False, is_transpose=True)
+                    nc.tensor.matmul(bank[:, j, :], lhsT=pred_rep[:, ug * K + j * P:ug * K + (j + 1) * P], rhs=ident[:], start=False, stop=True, is_transpose=True)
 
         def tanh(s):
             vs, ts = steps[s]
             n = len(vs) + len(ts)
             joint = joints.tile([P, n * P, 4], BF16, name="joint", tag="joint%d" % n, align_bytes=64)
             joint_t[s] = joint
-            if vs:
-                nc.scalar.activation(out=joint[:, 0:len(vs) * P, :].rearrange("p (c i) j -> p c j i", i=4), in_=sum_t[s][:].rearrange("p j (c i) -> p c j i", i=4), func=TANH)
+            plane = planes.tile([P, 4, len(vs) * P], BF16, name="plane", tag="plane%d" % len(vs), align_bytes=64)
+            plane_t[s] = plane
+            for i, (b, u) in enumerate(vs):
+                for j in range(4):
+                    nc.scalar.activation(out=plane[:, j, i * P:(i + 1) * P], in_=encT[:, b, j, :], func=TANH, bias=predT[:, j, b * U + u:b * U + u + 1])
             for i, bank in enumerate(bank_t[s]):
                 r = (len(vs) + i) * P
                 nc.scalar.activation(out=joint[:, r:r + P, :], in_=bank[:].rearrange("p j n -> p n j"), func=TANH)
+
+        def interleave(s):
+            nv = len(steps[s][0])
+            nc.vector.tensor_copy(out=joint_t[s][:, 0:nv * P, :].rearrange("p (c i) j -> p c j i", i=4), in_=plane_t[s][:].rearrange("p j (c i) -> p c j i", i=4))
 
         def quantize(s):
             n = sum(len(x) for x in steps[s])
@@ -249,41 +246,37 @@ def tile_jointnetwork_t_w4_kernel(tc, enc_bytes, enc_scale, pred, w_enc, s_enc, 
             col = 0
             while vs or ts:
                 units = vs or ts
-                block = U if vs else 4
                 n = 1
-                while n < len(units) and units[n] // block == units[0] // block:
+                while n < len(units) and units[n] == (units[0][0], units[0][1] + n):
                     n += 1
-                b, u0 = divmod(units[0], U)
                 if vs:
-                    dst = out[b, :, u0:u0 + n, :]
+                    b, u = vs[0]
+                    dst = out[b, :, u:u + n, :]
                     vs = vs[n:]
                 else:
-                    tg, ug = divmod(u0, 4)
-                    dst = out[b].rearrange("(a g) (c h) v -> g a c h v", g=8, h=4)[tg][:, :, ug:ug + n, :]
+                    tg, ug = ts[0]
+                    dst = out[B - 1].rearrange("(a g) (c h) v -> g a c h v", g=8, h=4)[tg][:, :, ug:ug + n, :]
                     ts = ts[n:]
                 nc.sync.dma_start(out=dst, in_=res_t[s][:, col:col + n, :])
                 col += n
 
-        work = {0: [(2, 2)], 1: [(2, 3)], 6: [(1, 0)], 7: [(1, 1)], 8: [(1, 2)], 9: [(1, 3)], 12: [(3, 0)], 13: [(3, 1)], 14: [(3, 2)], 15: [(3, 3)]}
-        prepare(2, 0, None)
-        adds(0, 0)
-        prepare(2, 1, nc.scalar.copy)
+        work = {0: [(3, 2)], 1: [(3, 3)], 6: [(1, 0)], 7: [(1, 1)], 8: [(1, 2)], 9: [(1, 3)], 13: [(2, 0)], 14: [(2, 1)], 15: [(2, 2)], 16: [(2, 3)]}
+        prepare(3, 0, None)
+        prepare(3, 1, nc.scalar.copy)
         tensor_sums(0)
         for s in range(n_steps + 2):
             if s < n_steps:
                 tanh(s)
-            if s + 1 < n_steps:
-                adds(s + 1, 0)
+            if 1 <= s <= n_steps:
+                interleave(s - 1)
             for b, stage in work.get(s, []):
-                prepare(b, stage, nc.scalar.copy if b == 2 else nc.vector.tensor_copy)
+                prepare(b, stage, nc.scalar.copy)
             if s + 1 < n_steps:
                 tensor_sums(s + 1)
+            if s >= 2:
+                add_bias(s - 2)
             if 1 <= s <= n_steps:
                 quantize(s - 1)
                 multiply(s - 1)
-            if s >= 2:
-                add_bias(s - 2)
-            if s + 1 < n_steps:
-                adds(s + 1, 1)
             if s >= 2:
                 clip_store(s - 2)

from contextlib import ExitStack

import concourse.mybir as mybir
from concourse.masks import make_identity

F32 = mybir.dt.float32
BF16 = mybir.dt.bfloat16
I32 = mybir.dt.int32
U32 = mybir.dt.uint32
U8 = mybir.dt.uint8
FP8 = mybir.dt.float8_e4m3fn
FP8X4 = mybir.dt.float8_e4m3fn_x4
FP4X4 = mybir.dt.float4_e2m1fn_x4
ADD = mybir.AluOpType.add
MULT = mybir.AluOpType.mult
MIN = mybir.AluOpType.min
MAX = mybir.AluOpType.max
TANH = mybir.ActivationFunctionType.Tanh

P = 128
B, T, U, K, V = 4, 128, 32, 512, 128
LIM = 15.0
FLOPS = 2 * K * (B * T * K + B * U * K + B * T * U * V)


def tile_jointnetwork_t_w4_kernel(tc, enc_bytes, enc_scale, pred, w_enc, s_enc, b_enc, w_pred, s_pred, b_pred, w_out, s_out, b_out, out):
    nc = tc.nc
    with ExitStack() as ctx:
        keep = ctx.enter_context(tc.tile_pool(name="keep", bufs=1))
        head = ctx.enter_context(tc.tile_pool(name="head", bufs=2))
        planes = ctx.enter_context(tc.tile_pool(name="planes", bufs=3))
        joints = ctx.enter_context(tc.tile_pool(name="joints", bufs=3))
        results = ctx.enter_context(tc.tile_pool(name="results", bufs=4))
        psum = ctx.enter_context(tc.psum_pool(name="psum", bufs=8))
        ctx.enter_context(tc.manual_schedule())

        ident = keep.tile([P, P], F32, name="ident")
        make_identity(nc, ident[:])

        scale_bc = keep.tile([P, K], F32, name="scale_bc")
        pred_in = keep.tile([P, K], BF16, name="pred_in")
        codes_in = keep.tile([P, B, K], U8, name="codes_in")
        wp_raw = keep.tile([P, 2 * K], U8, name="wp_raw", align_bytes=64)
        we_raw = keep.tile([P, 2 * K], U8, name="we_raw", align_bytes=64)
        sp_raw = keep.tile([P, K], U8, name="sp_raw", align_bytes=64)
        se_raw = keep.tile([P, K], U8, name="se_raw", align_bytes=64)
        wo = keep.tile([P, 2 * V], U8, name="wo", align_bytes=64)
        so = keep.tile([P, V], U8, name="so", align_bytes=64)
        bias_e = keep.tile([P, 4], BF16, name="bias_e")
        bias_p = keep.tile([P, 4], BF16, name="bias_p")
        bias_o = keep.tile([P, V], BF16, name="bias_o")

        def load_scales(dst, src, n):
            rows = src[0].rearrange("(q r) n -> r q n", r=4).bitcast(I32)
            for r in range(4):
                nc.sync.dma_start(out=dst[r:P:4, :].bitcast(I32), in_=rows[r].unsqueeze(1).to_broadcast([4, 8, n // 4]))

        nc.scalar.dma_start(out=pred_in[:], in_=pred.rearrange("b u k -> (b u) k"))
        nc.scalar.dma_start(out=scale_bc[:], in_=enc_scale.rearrange("a b k -> (a b k)").partition_broadcast(P))
        nc.sync.dma_start(out=codes_in[:, 0:B:3, :], in_=enc_bytes[0:B:3].rearrange("b t k -> t b k"))
        nc.sync.dma_start(out=wp_raw[:], in_=w_pred[0])
        load_scales(sp_raw, s_pred, K)
        nc.sync.dma_start(out=we_raw[:], in_=w_enc[0])
        load_scales(se_raw, s_enc, K)
        nc.gpsimd.dma_start(out=bias_e[:], in_=b_enc.rearrange("(p j) -> p j", j=4))
        nc.gpsimd.dma_start(out=bias_p[:], in_=b_pred.rearrange("(p j) -> p j", j=4))
        nc.sync.dma_start(out=codes_in[:, 1:3, :], in_=enc_bytes[1:3].rearrange("b t k -> t b k"))
        nc.sync.dma_start(out=wo[:], in_=w_out[0])
        load_scales(so, s_out, V)

        dummy = keep.tile([P, 1], F32, name="dummy")
        nc.vector.memset(dummy[:], 0.0)
        dummy_o = keep.tile([P, 1], F32, name="dummy_o")
        nc.scalar.activation(out=dummy_o[:], in_=dummy[:], func=TANH)
        nc.gpsimd.dma_start(out=bias_o[:], in_=b_out.partition_broadcast(P))

        wp = keep.tile([P, 2 * K], U8, name="wp", align_bytes=64)
        we = keep.tile([P, 2 * K], U8, name="we", align_bytes=64)
        sp = keep.tile([P, K], U8, name="sp", align_bytes=64)
        se = keep.tile([P, K], U8, name="se", align_bytes=64)
        bias = keep.tile([P, 4], F32, name="bias")
        x_enc = keep.tile([P, B, K], BF16, name="x_enc")
        predT = keep.tile([P, 4, P], F32, name="predT")
        encT = keep.tile([P, 3, 4, P], F32, name="encT")
        encR = keep.tile([P, K], F32, name="encR")
        pred_rows = keep.tile([P, K], F32, name="pred_rows")

        def permute_words(dst, src):
            nc.vector.tensor_copy(out=dst[:].rearrange("p (j m c) -> p j m c", j=4, c=2), in_=src[:].rearrange("p (m j c) -> p j m c", j=4, c=2))

        def permute_scales(dst, src):
            nc.vector.tensor_copy(out=dst[:].rearrange("p (j m) -> p j m", j=4), in_=src[:].rearrange("p (m j) -> p j m", j=4))

        def widen(b):
            nc.vector.tensor_tensor(out=x_enc[:, b, :], in0=codes_in[:, b, :].bitcast(FP8), in1=scale_bc[:], op=MULT)

        def turn(rows):
            words = rows.bitcast(F32)
            xt = psum.tile([P, 2, P], F32, name="xt", tag="bank")
            for u in range(2):
                nc.tensor.transpose(xt[:, u, :], words[:, u:2 * P:2], ident[:])
            return xt

        def group(copy, xt):
            grouped = head.tile([P, P, 4], BF16, name="grouped", align_bytes=64)
            copy(out=grouped[:].rearrange("p r j -> p (r j)").bitcast(F32).rearrange("p (r u) -> p r u", u=2), in_=xt[:].rearrange("p u r -> p r u"))
            return grouped

        def quant(grouped):
            q = head.tile([P, P], U32, name="q", align_bytes=64)
            qs = head.tile([P, P], U8, name="qs", align_bytes=64)
            nc.vector.quantize_mx(out=q[:].bitcast(FP8X4), scales=qs[:], in_=grouped[:].rearrange("p r j -> p (r j)"))
            return q, qs

        def project(w, s, q, qs):
            acc = psum.tile([P, 4, P], F32, name="acc", tag="bank")
            for j in range(4):
                nc.tensor.matmul_mx(out=acc[:, j, :], lhsT=w[:, 2 * P * j:2 * P * (j + 1)].bitcast(FP4X4), lhsT_scale=s[:, P * j:P * (j + 1)], rhs=q[:].bitcast(FP8X4), rhs_scale=qs[:], start=True, stop=True)
            return acc

        def project_rows(q, qs):
            acc = psum.tile([P, K], F32, name="racc", tag="bank")
            nc.tensor.matmul_mx(out=acc[:], lhsT=q[:].bitcast(FP8X4), lhsT_scale=qs[:], rhs=we[:].bitcast(FP4X4), rhs_scale=se[:], start=True, stop=True)
            return acc

        xt = turn(pred_in[:])
        g_pred = group(nc.scalar.copy, xt)
        widen(0)
        permute_words(wp, wp_raw)
        permute_scales(sp, sp_raw)
        q_pred = quant(g_pred)
        xt = turn(x_enc[:, 0, :])
        g_enc = group(nc.scalar.copy, xt)
        acc_p = project(wp, sp, *q_pred)
        nc.vector.tensor_tensor(out=bias[:], in0=bias_e[:], in1=bias_p[:], op=ADD)
        permute_words(we, we_raw)
        permute_scales(se, se_raw)
        q_enc = quant(g_enc)
        nc.vector.tensor_tensor(out=predT[:], in0=acc_p[:], in1=bias[:].unsqueeze(2).to_broadcast([P, 4, P]), op=ADD)
        acc = project(we, se, *q_enc)
        nc.scalar.copy(out=encT[:, 0], in_=acc[:])

        back = psum.tile([P, 4, P], F32, name="back", tag="bank")
        for j in range(4):
            nc.tensor.transpose(back[:, j, :], predT[:, j, :], ident[:])
        nc.scalar.copy(out=pred_rows[:], in_=back[:].rearrange("p j m -> p (j m)"))
        enc_scratch = out[B - 1, 0:16].rearrange("t u v -> (t u v)")
        pred_scratch = out[B - 1, 16:20].rearrange("t u v -> (t u v)")
        nc.sync.dma_start(out=pred_scratch.rearrange("(p k) -> p k", k=K), in_=pred_rows[3 * U:4 * U, :])
        enc_rep = keep.tile([P, 8 * K], F32, name="enc_rep")
        pred_rep = keep.tile([P, 4 * K], F32, name="pred_rep")

        def load_pred_rep(lo, hi):
            src = pred_scratch.rearrange("(c n) -> c n", c=8)
            nc.sync.dma_start(out=pred_rep[:, lo * K:hi * K], in_=src[:, lo * K:hi * K].unsqueeze(0).to_broadcast([16, 8, (hi - lo) * K]))

        def load_enc_rep(lo, hi):
            src = enc_scratch.rearrange("(a n) -> a n", a=16)
            nc.sync.dma_start(out=enc_rep[:, lo * K:hi * K], in_=src[:, lo * K:hi * K].unsqueeze(1).to_broadcast([16, 8, (hi - lo) * K]))

        load_pred_rep(0, 2)

        prep = {}

        def prepare(b, stage, copy):
            if stage == 0:
                widen(b)
                prep[b] = turn(x_enc[:, b, :])
            elif stage == 1:
                prep[b] = group(copy, prep[b])
            elif stage == 2:
                q = quant(prep[b])
                prep[b] = project(we, se, *q) if b < 3 else project_rows(*q)
            elif b < 3:
                copy(out=encT[:, b], in_=prep[b][:])
            else:
                copy(out=encR[:], in_=prep[b][:])
                nc.sync.dma_start(out=enc_scratch.rearrange("(p k) -> p k", k=K), in_=encR[:])
                load_enc_rep(0, 1)
                load_pred_rep(2, 4)
                load_enc_rep(1, 8)

        shape = [(1, 0), (1, 0), (2, 0), (4, 0), (4, 0)]
        for i in range(28):
            shape.append((2, 2) if i in (8, 16, 24) else (3, 1))
        shape += [(1, 1), (1, 0), (1, 0)]
        v_units = [(b, u) for b in range(3) for u in range(U)]
        t_units = [(tg, ug) for tg in range(8) for ug in range(4)]
        steps = []
        for nv, nt in shape:
            steps.append((v_units[:nv], t_units[:nt]))
            v_units, t_units = v_units[nv:], t_units[nt:]
        assert not v_units and not t_units, (len(v_units), len(t_units))
        n_steps = len(steps)
        bank_t, plane_t, joint_t, code_t, acc_t, res_t = {}, {}, {}, {}, {}, {}

        def tensor_sums(s):
            bank_t[s] = []
            for tg, ug in steps[s][1]:
                bank = psum.tile([P, 4, P], F32, name="tsum", tag="bank")
                bank_t[s].append(bank)
                for j in range(4):
                    nc.tensor.matmul(bank[:, j, :], lhsT=enc_rep[:, tg * K + j * P:tg * K + (j + 1) * P], rhs=ident[:], start=True, stop=False, is_transpose=True)
                    nc.tensor.matmul(bank[:, j, :], lhsT=pred_rep[:, ug * K + j * P:ug * K + (j + 1) * P], rhs=ident[:], start=False, stop=True, is_transpose=True)

        def tanh(s):
            vs, ts = steps[s]
            n = len(vs) + len(ts)
            joint = joints.tile([P, n * P, 4], BF16, name="joint", tag="joint%d" % n, align_bytes=64)
            joint_t[s] = joint
            plane = planes.tile([P, 4, len(vs) * P], BF16, name="plane", tag="plane%d" % len(vs), align_bytes=64)
            plane_t[s] = plane
            for i, (b, u) in enumerate(vs):
                for j in range(4):
                    nc.scalar.activation(out=plane[:, j, i * P:(i + 1) * P], in_=encT[:, b, j, :], func=TANH, bias=predT[:, j, b * U + u:b * U + u + 1])
            for i, bank in enumerate(bank_t[s]):
                r = (len(vs) + i) * P
                nc.scalar.activation(out=joint[:, r:r + P, :], in_=bank[:].rearrange("p j n -> p n j"), func=TANH)

        def interleave(s):
            nv = len(steps[s][0])
            nc.vector.tensor_copy(out=joint_t[s][:, 0:nv * P, :].rearrange("p (c i) j -> p c j i", i=4), in_=plane_t[s][:].rearrange("p j (c i) -> p c j i", i=4))

        def quantize(s):
            n = sum(len(x) for x in steps[s])
            q = joints.tile([P, n * P], U32, name="jq", tag="jq%d" % n, align_bytes=64)
            qs = joints.tile([P, n * P], U8, name="jqs", tag="jqs%d" % n, align_bytes=64)
            nc.vector.quantize_mx(out=q[:].bitcast(FP8X4), scales=qs[:], in_=joint_t[s][:].rearrange("p n j -> p (n j)"))
            code_t[s] = (q, qs, n)

        def multiply(s):
            q, qs, n = code_t[s]
            acc_t[s] = psum.tile([P, n, V], F32, name="oacc", tag="bank")
            for u in range(n):
                nc.tensor.matmul_mx(out=acc_t[s][:, u, :], lhsT=q[:, u * P:(u + 1) * P].bitcast(FP8X4), lhsT_scale=qs[:, u * P:(u + 1) * P], rhs=wo[:].bitcast(FP4X4), rhs_scale=so[:], start=True, stop=True)

        def add_bias(s):
            n = code_t[s][2]
            res_t[s] = results.tile([P, 4, V], F32, name="res")
            nc.vector.tensor_tensor(out=res_t[s][:, 0:n, :], in0=acc_t[s][:], in1=bias_o[:].unsqueeze(1).to_broadcast([P, n, V]), op=ADD)

        def clip_store(s):
            n = code_t[s][2]
            nc.vector.tensor_scalar(out=res_t[s][:, 0:n, :], in0=res_t[s][:, 0:n, :], scalar1=LIM, scalar2=-LIM, op0=MIN, op1=MAX)
            vs, ts = steps[s]
            col = 0
            while vs or ts:
                units = vs or ts
                n = 1
                while n < len(units) and units[n] == (units[0][0], units[0][1] + n):
                    n += 1
                if vs:
                    b, u = vs[0]
                    dst = out[b, :, u:u + n, :]
                    vs = vs[n:]
                else:
                    tg, ug = ts[0]
                    dst = out[B - 1].rearrange("(a g) (c h) v -> g a c h v", g=8, h=4)[tg][:, :, ug:ug + n, :]
                    ts = ts[n:]
                nc.sync.dma_start(out=dst, in_=res_t[s][:, col:col + n, :])
                col += n

        work = {0: [(3, 2)], 1: [(3, 3)], 6: [(1, 0)], 7: [(1, 1)], 8: [(1, 2)], 9: [(1, 3)], 13: [(2, 0)], 14: [(2, 1)], 15: [(2, 2)], 16: [(2, 3)]}
        prepare(3, 0, None)
        prepare(3, 1, nc.scalar.copy)
        tensor_sums(0)
        for s in range(n_steps + 2):
            if s < n_steps:
                tanh(s)
            if 1 <= s <= n_steps:
                interleave(s - 1)
            for b, stage in work.get(s, []):
                prepare(b, stage, nc.scalar.copy)
            if s + 1 < n_steps:
                tensor_sums(s + 1)
            if s >= 2:
                add_bias(s - 2)
            if 1 <= s <= n_steps:
                quantize(s - 1)
                multiply(s - 1)
            if s >= 2:
                clip_store(s - 2)
